import numpy as np
import ml_dtypes


def mxq(x, axis, fmt="e4m3"):
    dtype, down = {"e4m3": (ml_dtypes.float8_e4m3fn, 7), "e5m2": (ml_dtypes.float8_e5m2, 14)}[fmt]
    v = np.moveaxis(np.asarray(x, np.float32).astype(ml_dtypes.bfloat16).astype(np.float64), axis, -1)
    blocks = v.reshape(v.shape[:-1] + (-1, 32))
    amax = np.abs(blocks).max(-1, keepdims=True)
    byte = np.maximum(np.where(amax > 0, np.frexp(amax)[1] - 1 + 127, 0) - down, 1)
    scale = np.exp2(byte - 127.0)
    codes = (blocks / scale).astype(np.float32).astype(dtype).astype(np.float64)
    return np.moveaxis((codes * scale).reshape(v.shape), -1, axis)


WIDE = False


def mx_kscale(k):
    if not WIDE:
        return np.ones(k)
    levels = np.array([10, -10, 5, -5, 0])
    a = np.random.permutation(np.resize(levels, k // 512 * 4)).reshape(k // 512, 4)
    idx = np.arange(k)
    return np.exp2(a[idx // 512, idx % 128 // 32])


BF16 = ml_dtypes.bfloat16


def bf(x):
    return np.asarray(x, np.float32).astype(BF16)


def f64(x):
    return np.asarray(x).astype(np.float64)


B, S, D_MODEL, H, NOPE, ROPE = 1, 512, 2048, 4, 256, 128
DK = D_MODEL // H
LAT = 3 * DK
D_HEAD = NOPE + ROPE
D_LATENT = H * D_HEAD
ROT_DIM = 2 * ((ROPE // 2) // 2)
EPS = 1e-6


def rmsnorm(x, w):
    return x * (1.0 / np.sqrt(np.mean(x * x, axis=-1, keepdims=True) + EPS)) * w


def apply_rope(x):
    inv_freq = 1.0 / (10000.0 ** (np.arange(0, ROT_DIM, 2) / ROT_DIM))
    freqs = np.arange(x.shape[-2])[:, None] * inv_freq[None, :]
    freqs = np.repeat(freqs, 2, axis=-1)
    cos, sin = np.cos(freqs), np.sin(freqs)
    xl, xr = x[..., :ROT_DIM], x[..., ROT_DIM:]
    x1, x2 = xl[..., 0::2], xl[..., 1::2]
    rot = np.stack([-x2, x1], axis=-1).reshape(xl.shape)
    return np.concatenate([xl * cos + rot * sin, xr], axis=-1)


def to_heads(t):
    return t.reshape(B, S, D_HEAD, H).transpose(0, 3, 1, 2)


def setup_inputs():
    s, t = mx_kscale(D_MODEL), mx_kscale(LAT)
    return {"x": bf(np.random.standard_normal((B, S, D_MODEL)) * s),
            "w_down": bf(np.random.standard_normal((D_MODEL, LAT)) / np.sqrt(D_MODEL) / s[:, None]),
            "rms_w": bf((1.0 + 0.1 * np.random.standard_normal(LAT)) * t),
            "w_up": bf(np.random.standard_normal((LAT, 3 * D_LATENT)) * 1.25 / np.sqrt(LAT) / t[:, None])}


def reference(x, w_down, rms_w, w_up):
    h = mxq(f64(x), 2, "e4m3") @ mxq(f64(w_down), 0, "e4m3")
    h = rmsnorm(h, f64(rms_w))
    qkv = mxq(h, 2, "e4m3") @ mxq(f64(w_up), 0, "e4m3")
    q, k, v = np.split(qkv, 3, axis=-1)
    q, k, v = to_heads(q), to_heads(k), to_heads(v)
    q_nope, q_rope = q[..., :NOPE], q[..., NOPE:]
    k_nope, k_rope = k[..., :NOPE], k[..., NOPE:]
    q_rope = apply_rope(q_rope)
    k_rope = apply_rope(k_rope)
    return (np.ascontiguousarray(q_nope), q_rope, np.ascontiguousarray(k_nope), k_rope, np.ascontiguousarray(v))

@@ -1,0 +1,457 @@
+from contextlib import ExitStack
+
+import concourse.mybir as mybir
+from concourse.masks import make_identity
+
+F32 = mybir.dt.float32
+BF16 = mybir.dt.bfloat16
+I32 = mybir.dt.int32
+U32 = mybir.dt.uint32
+U8 = mybir.dt.uint8
+FP8X4 = mybir.dt.float8_e4m3fn_x4
+ALU = mybir.AluOpType
+ACT = mybir.ActivationFunctionType
+AXIS = mybir.AxisListType
+
+P = 128
+PACK = 4
+K_PASS = P * PACK
+BANK = 512
+PSUM_BANKS = 8
+
+TOKENS = 512
+TOKEN_TILES = TOKENS // P
+TOKEN_PAIRS = TOKEN_TILES // 2
+D_MODEL = 2048
+LATENT = 1536
+HEADS = 4
+NOPE = 256
+ROPE = 128
+ROTATED = 64
+PAIRS = ROTATED // 2
+D_HEAD = NOPE + ROPE
+THIRD = HEADS * D_HEAD
+THIRDS = 3
+EPS = 1e-6
+
+DOWN_PASSES = D_MODEL // K_PASS
+UP_PASSES = LATENT // K_PASS
+BLOCKS = LATENT // BANK
+CHUNKS = DOWN_PASSES + THIRDS * UP_PASSES
+RAW_BUFS = 5
+FETCH_AHEAD = 3
+TWO_PI = 6.283185307179586
+ROUND_MAGIC = 12582912.0
+
+FLOPS = 2 * TOKENS * (D_MODEL * LATENT + LATENT * THIRDS * THIRD)
+
+
+def tile_mhlattention_pa_kernel(tc, x, w_down, rms_w, w_up, out_0, out_1, out_2, out_3, out_4):
+    nc = tc.nc
+    with ExitStack() as pools:
+        pools.enter_context(tc.manual_schedule())
+        consts = pools.enter_context(tc.tile_pool(name="consts", bufs=1))
+        raw_pool = pools.enter_context(tc.tile_pool(name="raw", bufs=RAW_BUFS))
+        grouped_pool = pools.enter_context(tc.tile_pool(name="grouped", bufs=2 * BLOCKS))
+        up_pool = pools.enter_context(tc.tile_pool(name="up", bufs=2))
+        keep = pools.enter_context(tc.tile_pool(name="keep", bufs=1))
+        norm_pool = pools.enter_context(tc.tile_pool(name="norm", bufs=2))
+        banks = pools.enter_context(tc.psum_pool(name="banks", bufs=PSUM_BANKS))
+
+        def new_bank(shape, dtype, name):
+            return banks.tile(shape, dtype, name=name, tag="bank")
+
+        ident_f32 = consts.tile([P, P], F32, name="ident_f32")
+        make_identity(nc, ident_f32[:])
+        ident_bf = consts.tile([P, P], BF16, name="ident_bf")
+        make_identity(nc, ident_bf[:])
+        gain = consts.tile([P, LATENT], BF16, name="gain")
+
+        pos_int = consts.tile([P, TOKEN_TILES], I32, name="pos_int")
+        nc.gpsimd.iota(pos_int[:], pattern=[[1, TOKEN_TILES]], base=0, channel_multiplier=TOKEN_TILES)
+        pos = consts.tile([P, TOKEN_TILES], F32, name="pos")
+        turns = consts.tile([P, 2, PAIRS, TOKEN_TILES], F32, name="turns")
+        whole = consts.tile([P, 2, PAIRS, TOKEN_TILES], F32, name="whole")
+        frac = consts.tile([P, 2, PAIRS, TOKEN_TILES], F32, name="frac")
+        trig = consts.tile([P, 2, PAIRS, TOKEN_TILES], F32, name="trig")
+        cos_rep = consts.tile([P, TOKEN_TILES, PAIRS, 2], F32, name="cos_rep")
+        sin_sign = consts.tile([P, TOKEN_TILES, 2, PAIRS], F32, name="sin_sign")
+
+        def angles():
+            nc.vector.tensor_copy(out=pos[:], in_=pos_int[:])
+            for i in range(PAIRS):
+                nc.vector.tensor_scalar_mul(
+                    out=turns[:, 0, i, :], in0=pos[:], scalar1=10000.0 ** (-i / PAIRS) / TWO_PI
+                )
+            nc.vector.tensor_scalar_add(out=turns[:, 1, :, :], in0=turns[:, 0, :, :], scalar1=0.25)
+            nc.vector.tensor_scalar(
+                out=whole[:], in0=turns[:], scalar1=ROUND_MAGIC, scalar2=ROUND_MAGIC, op0=ALU.add, op1=ALU.subtract
+            )
+            nc.vector.tensor_tensor(out=frac[:], in0=turns[:], in1=whole[:], op=ALU.subtract)
+            nc.scalar.activation(out=trig[:], in_=frac[:], func=ACT.Sin, scale=TWO_PI)
+
+        def rope_tables():
+            nc.vector.tensor_copy(
+                out=cos_rep[:],
+                in_=trig[:, 1, :, :]
+                .rearrange("p i t -> p t i")
+                .unsqueeze(3)
+                .to_broadcast([P, TOKEN_TILES, PAIRS, 2]),
+            )
+            nc.vector.tensor_scalar_mul(
+                out=sin_sign[:, :, 0, :], in0=trig[:, 0, :, :].rearrange("p i t -> p t i"), scalar1=-1.0
+            )
+            nc.vector.tensor_copy(out=sin_sign[:, :, 1, :], in_=trig[:, 0, :, :].rearrange("p i t -> p t i"))
+
+        n_grouped = keep.tile([P, UP_PASSES, TOKEN_TILES, P * PACK], BF16, name="n_grouped", align_bytes=64)
+        n_codes = keep.tile([P, UP_PASSES, TOKEN_TILES, P], U32, name="n_codes", align_bytes=64)
+        n_scales = keep.tile([P, UP_PASSES, TOKEN_TILES, P], U8, name="n_scales", align_bytes=64)
+        sum_sq = keep.tile([P, TOKEN_TILES, BLOCKS], F32, name="sum_sq")
+        sum_copy = keep.tile([P, TOKEN_TILES, BLOCKS], F32, name="sum_copy")
+        total_sq = keep.tile([P, TOKEN_TILES], F32, name="total_sq")
+        rms = keep.tile([P, TOKEN_TILES], F32, name="rms")
+        rstd = keep.tile([P, TOKEN_TILES], F32, name="rstd")
+
+
+        up_codes = {}
+        up_scales = {}
+        chunk_raw = {}
+        chunk_target = {}
+        chunk_grouped = {}
+
+        def fetch(s):
+            if s >= CHUNKS:
+                return
+            raw = raw_pool.tile([P, PACK, LATENT], BF16, name="raw", tag="raw")
+            if s < DOWN_PASSES:
+                pieces = BLOCKS if s == 0 else 1
+                width = LATENT // pieces
+                for piece in range(pieces):
+                    cols = slice(width * piece, width * (piece + 1))
+                    for u in range(2):
+                        rows = w_down[K_PASS * s + 256 * u : K_PASS * s + 256 * (u + 1), cols]
+                        nc.sync.dma_start(
+                            out=raw[:, 2 * u : 2 * u + 2, cols], in_=rows.rearrange("(q e) c -> q e c", e=2)
+                        )
+                chunk_target[s] = (down_codes[:, s, :], down_scales[:, s, :])
+            else:
+                third, g = divmod(s - DOWN_PASSES, UP_PASSES)
+                if g == 0:
+                    up_codes[third] = up_pool.tile(
+                        [P, UP_PASSES, THIRD], U32, name="up_codes", tag="up_codes", align_bytes=64
+                    )
+                    up_scales[third] = up_pool.tile(
+                        [P, UP_PASSES, THIRD], U8, name="up_scales", tag="up_scales", align_bytes=64
+                    )
+                rows = w_up[K_PASS * g : K_PASS * (g + 1), THIRD * third : THIRD * (third + 1)]
+                nc.sync.dma_start(out=raw[:], in_=rows.rearrange("(j p) c -> p j c", p=P))
+                chunk_target[s] = (up_codes[third][:, g, :], up_scales[third][:, g, :])
+            chunk_raw[s] = raw
+
+        def scalar_blocks(s):
+            return 1
+
+        def regroup(s):
+            if s >= CHUNKS:
+                return
+            chunk_grouped[s] = []
+            for b in range(BLOCKS):
+                grouped = grouped_pool.tile([P, BANK * PACK], BF16, name="grouped", tag="grouped", align_bytes=64)
+                copy = nc.scalar.copy if b >= BLOCKS - scalar_blocks(s) else nc.vector.tensor_copy
+                copy(
+                    out=grouped[:].rearrange("p (c i t) -> p c t i", i=4, t=PACK),
+                    in_=chunk_raw[s][:, :, BANK * b : BANK * (b + 1)].rearrange("p t (c i) -> p c t i", i=4),
+                )
+                chunk_grouped[s].append(grouped)
+
+        def quantise(s):
+            codes, scales = chunk_target[s]
+            for b in range(BLOCKS):
+                cols = slice(BANK * b, BANK * (b + 1))
+                nc.vector.quantize_mx(
+                    out=codes[:, cols].bitcast(FP8X4), scales=scales[:, cols], in_=chunk_grouped[s][b][:]
+                )
+
+        def step(s):
+            fetch(s + FETCH_AHEAD)
+            regroup(s + 1)
+            quantise(s)
+
+        x_raw = {}
+
+        def fetch_x(pair):
+            x_raw[pair] = raw_pool.tile([P, 2, D_MODEL], BF16, name="x_raw", tag="raw")
+            nc.sync.dma_start(
+                out=x_raw[pair][:],
+                in_=x[0].rearrange("(p t) k -> p t k", t=TOKEN_TILES)[:, 2 * pair : 2 * pair + 2, :],
+            )
+
+        def quantise_x(pair):
+            for half in range(DOWN_PASSES // 2):
+                x_grouped = grouped_pool.tile([P, BANK * PACK], BF16, name="x_grouped", tag="grouped", align_bytes=64)
+                x_words = x_grouped[:].bitcast(F32).rearrange("q (g t u) -> q g t u", g=2, u=2)
+                for gg in range(2):
+                    g = 2 * half + gg
+                    flipped = new_bank([P, 2, 2 * P], F32, "x_flipped")
+                    for u in range(2):
+                        for tl in range(2):
+                            first_word = 256 * g + P * u
+                            nc.tensor.transpose(
+                                flipped[:, u, P * tl : P * (tl + 1)],
+                                x_raw[pair][:, tl, :].bitcast(F32)[:, first_word : first_word + P],
+                                ident_f32[:],
+                            )
+                    nc.scalar.copy(out=x_words[:, gg, :, :], in_=flipped[:].rearrange("q u t -> q t u"))
+                passes = slice(2 * half, 2 * half + 2)
+                nc.vector.quantize_mx(
+                    out=x_codes[:, pair, passes, :].rearrange("q g t -> q (g t)").bitcast(FP8X4),
+                    scales=x_scales[:, pair, passes, :].rearrange("q g t -> q (g t)"),
+                    in_=x_grouped[:],
+                )
+
+        h_banks = {}
+
+        def open_h_banks(pair):
+            for t in (2 * pair, 2 * pair + 1):
+                for b in range(BLOCKS):
+                    h_banks[(t, b)] = new_bank([P, BANK], F32, "h_bank")
+
+        def first_pass(t, b, g):
+            pair, tl = divmod(t, 2)
+            tok = slice(P * tl, P * (tl + 1))
+            cols = slice(BANK * b, BANK * (b + 1))
+            nc.tensor.matmul_mx(
+                out=h_banks[(t, b)][:],
+                lhsT=x_codes[:, pair, g, tok].bitcast(FP8X4),
+                lhsT_scale=x_scales[:, pair, g, tok],
+                rhs=down_codes[:, g, cols].bitcast(FP8X4),
+                rhs_scale=down_scales[:, g, cols],
+                start=(g == 0),
+                stop=(g == DOWN_PASSES - 1),
+            )
+
+        def squares(pair):
+            for t in (2 * pair, 2 * pair + 1):
+                for b in range(BLOCKS):
+                    unread = norm_pool.tile([P, BANK], BF16, name="unread", tag="unread", bufs=4)
+                    nc.scalar.activation(
+                        out=unread[:], in_=h_banks[(t, b)][:], func=ACT.Square, accum_out=sum_sq[:, t, b : b + 1]
+                    )
+                nc.scalar.activation(
+                    out=sum_copy[:, t, :], in_=sum_sq[:, t, :], func=ACT.Copy, accum_out=total_sq[:, t : t + 1]
+                )
+            two = slice(2 * pair, 2 * pair + 2)
+            nc.scalar.activation(out=rms[:, two], in_=total_sq[:, two], func=ACT.Sqrt, scale=1.0 / LATENT, bias=EPS)
+
+        n_bf = {}
+
+        def scale(pair):
+            two = slice(2 * pair, 2 * pair + 2)
+            nc.vector.reciprocal(out=rstd[:, two], in_=rms[:, two])
+            for t in (2 * pair, 2 * pair + 1):
+                n_bf[t] = norm_pool.tile([P, LATENT], BF16, name="n_bf", tag="n_bf", bufs=4)
+                for b in range(BLOCKS):
+                    cols = slice(BANK * b, BANK * (b + 1))
+                    nc.vector.scalar_tensor_tensor(
+                        out=n_bf[t][:, cols],
+                        in0=h_banks[(t, b)][:],
+                        scalar=rstd[:, t : t + 1],
+                        in1=gain[:, cols],
+                        op0=ALU.mult,
+                        op1=ALU.mult,
+                    )
+
+        def flip(pair):
+            for g in range(UP_PASSES):
+                flipped = new_bank([P, 2, PACK, P], BF16, "n_flipped")
+                for tl in range(2):
+                    for j in range(PACK):
+                        first_col = K_PASS * g + P * j
+                        nc.tensor.transpose(
+                            flipped[:, tl, j, :], n_bf[2 * pair + tl][:, first_col : first_col + P], ident_bf[:]
+                        )
+                nc.scalar.copy(
+                    out=n_grouped[:, g, 2 * pair : 2 * pair + 2, :].rearrange("p t (r j) -> p t r j", j=PACK),
+                    in_=flipped[:].rearrange("p t j r -> p t r j"),
+                )
+
+        def quantise_n(pair):
+            two = slice(2 * pair, 2 * pair + 2)
+            for g in range(UP_PASSES):
+                nc.vector.quantize_mx(
+                    out=n_codes[:, g, two, :].rearrange("p t r -> p (t r)").bitcast(FP8X4),
+                    scales=n_scales[:, g, two, :].rearrange("p t r -> p (t r)"),
+                    in_=n_grouped[:, g, two, :].rearrange("p t c -> p (t c)"),
+                )
+
+        outputs = [(out_0, out_1), (out_2, out_3), (out_4, None)]
+        staged = {}
+        split = 2 * HEADS * NOPE
+
+        qkv_banks = {}
+
+        def views(third):
+            if outputs[third][1] is None:
+                return staged[third][:].rearrange("p (h t d) -> p h t d", h=HEADS, t=2), None
+            return (
+                staged[third][:, 0:split].rearrange("p (h t d) -> p h t d", h=HEADS, t=2),
+                staged[third][:, split:].rearrange("p (h t d) -> p h t d", h=HEADS, t=2),
+            )
+
+        def open_bank(third, t, b):
+            if t % 2 == 0 and b == 0:
+                staged[third] = stage_pool.tile([P, 2 * THIRD], F32, name="staged", tag="staged")
+            qkv_banks[(t, b)] = new_bank([P, BANK], F32, "qkv_bank")
+
+        def second_pass(third, t, b, g):
+            cols = slice(BANK * b, BANK * (b + 1))
+            nc.tensor.matmul_mx(
+                out=qkv_banks[(t, b)][:],
+                lhsT=n_codes[:, g, t, :].bitcast(FP8X4),
+                lhsT_scale=n_scales[:, g, t, :],
+                rhs=up_codes[third][:, g, cols].bitcast(FP8X4),
+                rhs_scale=up_scales[third][:, g, cols],
+                start=(g == 0),
+                stop=(g == UP_PASSES - 1),
+            )
+
+        def drain(third, t, b, copy):
+            plain, rope = views(third)
+            if rope is not None and P * b >= NOPE:
+                target = rope[:, :, t % 2, :]
+            else:
+                target = plain[:, :, t % 2, P * b : P * (b + 1)]
+            copy(out=target, in_=qkv_banks[(t, b)][:].rearrange("p (d h) -> p h d", h=HEADS))
+
+        def second(third, t):
+            for b in range(BLOCKS):
+                open_bank(third, t, b)
+                for g in range(UP_PASSES):
+                    second_pass(third, t, b, g)
+                drain(third, t, b, nc.scalar.copy)
+
+        def store_plain(third, pair):
+            tokens = slice(2 * pair, 2 * pair + 2)
+            nc.sync.dma_start(
+                out=outputs[third][0][0].rearrange("h (p t) d -> p h t d", t=TOKEN_TILES)[:, :, tokens, :],
+                in_=views(third)[0],
+            )
+
+        def rotate(rope, pair, rope_out):
+            tokens = slice(2 * pair, 2 * pair + 2)
+            rotated = rope[:, :, :, 0:ROTATED]
+            partner = rotated.rearrange("p h t (i e) -> p h t i e", e=2)
+            swapped = swap_pool.tile([P, HEADS, 2, 2, PAIRS], F32, name="swapped", tag="swapped")
+            for e in range(2):
+                nc.vector.tensor_tensor(
+                    out=swapped[:, :, :, e, :],
+                    in0=partner[:, :, :, :, 1 - e],
+                    in1=sin_sign[:, tokens, e, :].unsqueeze(1).to_broadcast([P, HEADS, 2, PAIRS]),
+                    op=ALU.mult,
+                )
+            nc.vector.tensor_tensor(
+                out=rotated,
+                in0=rotated,
+                in1=cos_rep[:, tokens, :, :]
+                .rearrange("p t i e -> p t (i e)")
+                .unsqueeze(1)
+                .to_broadcast([P, HEADS, 2, ROTATED]),
+                op=ALU.mult,
+            )
+            rows = rotated.rearrange("p h t (i e) -> p (h t) i e", e=2)
+            nc.vector.tensor_tensor(
+                out=rows, in0=rows, in1=swapped[:].rearrange("p h t e i -> p (h t) i e"), op=ALU.add
+            )
+            nc.sync.dma_start(
+                out=rope_out[0].rearrange("h (p t) d -> p h t d", t=TOKEN_TILES)[:, :, tokens, :], in_=rope
+            )
+
+        with tc.tile_pool(name="first", bufs=1) as first_pool:
+            down_codes = first_pool.tile([P, DOWN_PASSES, LATENT], U32, name="down_codes", align_bytes=64)
+            down_scales = first_pool.tile([P, DOWN_PASSES, LATENT], U8, name="down_scales", align_bytes=64)
+            x_codes = first_pool.tile([P, TOKEN_PAIRS, DOWN_PASSES, 2 * P], U32, name="x_codes", align_bytes=64)
+            x_scales = first_pool.tile([P, TOKEN_PAIRS, DOWN_PASSES, 2 * P], U8, name="x_scales", align_bytes=64)
+            fetch(0)
+            fetch(1)
+            fetch_x(0)
+            fetch_x(1)
+            fetch(2)
+            nc.sync.dma_start(out=gain[:], in_=rms_w.partition_broadcast(P))
+            regroup(0)
+            angles()
+            step(0)
+            quantise_x(0)
+            rope_tables()
+            quantise_x(1)
+            open_h_banks(0)
+            for t in range(2):
+                for b in range(BLOCKS):
+                    first_pass(t, b, 0)
+            for g in range(1, DOWN_PASSES):
+                step(g)
+                for t in range(2):
+                    for b in range(BLOCKS):
+                        first_pass(t, b, g)
+            squares(0)
+            step(4)
+            scale(0)
+            flip(0)
+            open_h_banks(1)
+            for t in range(2, TOKEN_TILES):
+                for b in range(BLOCKS):
+                    for g in range(DOWN_PASSES):
+                        first_pass(t, b, g)
+        with tc.tile_pool(name="stage", bufs=4, reuse_waits="tile") as stage_pool, tc.tile_pool(
+            name="swap", bufs=2, reuse_waits="tile"
+        ) as swap_pool:
+            step(5)
+            quantise_n(0)
+            squares(1)
+            step(6)
+            scale(1)
+            second(0, 0)
+            second(0, 1)
+            flip(1)
+            step(7)
+            quantise_n(1)
+            store_plain(0, 0)
+            rotate(views(0)[1], 0, out_1)
+            second(0, 2)
+            step(8)
+            second(0, 3)
+            step(9)
+            store_plain(0, 1)
+            rotate(views(0)[1], 1, out_1)
+            second(1, 0)
+            second(1, 1)
+            store_plain(1, 0)
+            k_rope = {0: views(1)[1]}
+            step(10)
+            second(1, 2)
+            step(11)
+            second(1, 3)
+            store_plain(1, 1)
+            k_rope[1] = views(1)[1]
+            for t in range(2):
+                for b in range(BLOCKS):
+                    open_bank(2, t, b)
+                    for g in range(UP_PASSES - 1):
+                        second_pass(2, t, b, g)
+            step(12)
+            for b in range(BLOCKS):
+                for t in range(2):
+                    second_pass(2, t, b, UP_PASSES - 1)
+            for t in range(2):
+                for b in range(BLOCKS):
+                    drain(2, t, b, nc.vector.tensor_copy if (t * BLOCKS + b) % 2 == 0 else nc.scalar.copy)
+            store_plain(2, 0)
+            rotate(k_rope[0], 0, out_3)
+            for t in range(2, TOKEN_TILES):
+                for b in range(BLOCKS):
+                    open_bank(2, t, b)
+                    for g in range(UP_PASSES):
+                        second_pass(2, t, b, g)
+                    drain(2, t, b, nc.vector.tensor_copy if (t * BLOCKS + b) % 2 == 0 else nc.scalar.copy)
+                if t == 2:
+                    rotate(k_rope[1], 1, out_3)
+            store_plain(2, 1)

@@ -32,14 +32,16 @@ PAIRS = ROTATED // 2
 D_HEAD = NOPE + ROPE
 THIRD = HEADS * D_HEAD
 THIRDS = 3
+Q, K, V = 0, 1, 2
+TURN = (V, Q, K)
 EPS = 1e-6
 
 DOWN_PASSES = D_MODEL // K_PASS
 UP_PASSES = LATENT // K_PASS
 BLOCKS = LATENT // BANK
-CHUNKS = DOWN_PASSES + THIRDS * UP_PASSES
-RAW_BUFS = 5
-FETCH_AHEAD = 3
+LOADS = DOWN_PASSES + THIRDS * UP_PASSES
+STEPS = LOADS
+RAW_BUFS = 6
 TWO_PI = 6.283185307179586
 ROUND_MAGIC = 12582912.0
 
@@ -53,7 +55,7 @@ def tile_mhlattention_pa_kernel(tc, x, w_down, rms_w, w_up, out_0, out_1, out_2,
         consts = pools.enter_context(tc.tile_pool(name="consts", bufs=1))
         raw_pool = pools.enter_context(tc.tile_pool(name="raw", bufs=RAW_BUFS))
         grouped_pool = pools.enter_context(tc.tile_pool(name="grouped", bufs=2 * BLOCKS))
-        up_pool = pools.enter_context(tc.tile_pool(name="up", bufs=2))
+        up_pool = pools.enter_context(tc.tile_pool(name="up", bufs=4))
         keep = pools.enter_context(tc.tile_pool(name="keep", bufs=1))
         norm_pool = pools.enter_context(tc.tile_pool(name="norm", bufs=2))
         banks = pools.enter_context(tc.psum_pool(name="banks", bufs=PSUM_BANKS))
@@ -113,67 +115,86 @@ def tile_mhlattention_pa_kernel(tc, x, w_down, rms_w, w_up, out_0, out_1, out_2,
         rstd = keep.tile([P, TOKEN_TILES], F32, name="rstd")
 
 
+        raw_rows = {}
+        step_blocks = {}
+        step_grouped = {}
         up_codes = {}
         up_scales = {}
-        chunk_raw = {}
-        chunk_target = {}
-        chunk_grouped = {}
+        asked = [0]
 
-        def fetch(s):
-            if s >= CHUNKS:
+        def fetch_next():
+            load = asked[0]
+            asked[0] += 1
+            if load >= LOADS:
                 return
             raw = raw_pool.tile([P, PACK, LATENT], BF16, name="raw", tag="raw")
-            if s < DOWN_PASSES:
-                pieces = BLOCKS if s == 0 else 1
+            raw_rows[load] = raw
+            if load < DOWN_PASSES:
+                pieces = BLOCKS if load == 0 else 1
                 width = LATENT // pieces
                 for piece in range(pieces):
                     cols = slice(width * piece, width * (piece + 1))
                     for u in range(2):
-                        rows = w_down[K_PASS * s + 256 * u : K_PASS * s + 256 * (u + 1), cols]
+                        rows = w_down[K_PASS * load + 256 * u : K_PASS * load + 256 * (u + 1), cols]
                         nc.sync.dma_start(
                             out=raw[:, 2 * u : 2 * u + 2, cols], in_=rows.rearrange("(q e) c -> q e c", e=2)
                         )
-                chunk_target[s] = (down_codes[:, s, :], down_scales[:, s, :])
             else:
-                third, g = divmod(s - DOWN_PASSES, UP_PASSES)
-                if g == 0:
-                    up_codes[third] = up_pool.tile(
-                        [P, UP_PASSES, THIRD], U32, name="up_codes", tag="up_codes", align_bytes=64
-                    )
-                    up_scales[third] = up_pool.tile(
-                        [P, UP_PASSES, THIRD], U8, name="up_scales", tag="up_scales", align_bytes=64
-                    )
+                place, g = divmod(load - DOWN_PASSES, UP_PASSES)
+                third = TURN[place]
                 rows = w_up[K_PASS * g : K_PASS * (g + 1), THIRD * third : THIRD * (third + 1)]
                 nc.sync.dma_start(out=raw[:], in_=rows.rearrange("(j p) c -> p j c", p=P))
-                chunk_target[s] = (up_codes[third][:, g, :], up_scales[third][:, g, :])
-            chunk_raw[s] = raw
 
-        def scalar_blocks(s):
-            return 1
+        def blocks_of(s):
+            found = []
+            if s < DOWN_PASSES:
+                for b in range(BLOCKS):
+                    cols = slice(BANK * b, BANK * (b + 1))
+                    found.append((raw_rows[s][:, :, cols], down_codes[:, s, cols], down_scales[:, s, cols]))
+                return found
+            place, part = divmod(s - DOWN_PASSES, BLOCKS)
+            third = TURN[place]
+            for i in range(BLOCKS):
+                g, b = (part, i) if place == 0 else (i, part)
+                if (third, b) not in up_codes:
+                    up_codes[(third, b)] = up_pool.tile(
+                        [P, UP_PASSES, BANK], U32, name="up_codes", tag="up_codes", align_bytes=64
+                    )
+                    up_scales[(third, b)] = up_pool.tile(
+                        [P, UP_PASSES, BANK], U8, name="up_scales", tag="up_scales", align_bytes=64
+                    )
+                raw = raw_rows[DOWN_PASSES + UP_PASSES * place + g]
+                found.append(
+                    (raw[:, :, BANK * b : BANK * (b + 1)], up_codes[(third, b)][:, g, :], up_scales[(third, b)][:, g, :])
+                )
+            return found
 
         def regroup(s):
-            if s >= CHUNKS:
+            if s >= STEPS:
                 return
-            chunk_grouped[s] = []
-            for b in range(BLOCKS):
+            step_blocks[s] = blocks_of(s)
+            step_grouped[s] = []
+            for i in range(BLOCKS):
                 grouped = grouped_pool.tile([P, BANK * PACK], BF16, name="grouped", tag="grouped", align_bytes=64)
-                copy = nc.scalar.copy if b >= BLOCKS - scalar_blocks(s) else nc.vector.tensor_copy
+                copy = nc.scalar.copy if i == BLOCKS - 1 else nc.vector.tensor_copy
                 copy(
                     out=grouped[:].rearrange("p (c i t) -> p c t i", i=4, t=PACK),
-                    in_=chunk_raw[s][:, :, BANK * b : BANK * (b + 1)].rearrange("p t (c i) -> p c t i", i=4),
+                    in_=step_blocks[s][i][0].rearrange("p t (c i) -> p c t i", i=4),
                 )
-                chunk_grouped[s].append(grouped)
+                step_grouped[s].append(grouped)
+            if s < DOWN_PASSES + UP_PASSES:
+                fetch_next()
+            elif (s - DOWN_PASSES) % BLOCKS == BLOCKS - 1:
+                for g in range(UP_PASSES):
+                    fetch_next()
 
         def quantise(s):
-            codes, scales = chunk_target[s]
-            for b in range(BLOCKS):
-                cols = slice(BANK * b, BANK * (b + 1))
+            for i in range(BLOCKS):
                 nc.vector.quantize_mx(
-                    out=codes[:, cols].bitcast(FP8X4), scales=scales[:, cols], in_=chunk_grouped[s][b][:]
+                    out=step_blocks[s][i][1].bitcast(FP8X4), scales=step_blocks[s][i][2], in_=step_grouped[s][i][:]
                 )
 
         def step(s):
-            fetch(s + FETCH_AHEAD)
             regroup(s + 1)
             quantise(s)
 
@@ -290,54 +311,48 @@ def tile_mhlattention_pa_kernel(tc, x, w_down, rms_w, w_up, out_0, out_1, out_2,
 
         qkv_banks = {}
 
-        def views(third):
+        def views(third, pair):
+            whole_tile = staged[(third, pair)]
             if outputs[third][1] is None:
-                return staged[third][:].rearrange("p (h t d) -> p h t d", h=HEADS, t=2), None
+                return whole_tile[:].rearrange("p (h t d) -> p h t d", h=HEADS, t=2), None
             return (
-                staged[third][:, 0:split].rearrange("p (h t d) -> p h t d", h=HEADS, t=2),
-                staged[third][:, split:].rearrange("p (h t d) -> p h t d", h=HEADS, t=2),
+                whole_tile[:, 0:split].rearrange("p (h t d) -> p h t d", h=HEADS, t=2),
+                whole_tile[:, split:].rearrange("p (h t d) -> p h t d", h=HEADS, t=2),
             )
 
-        def open_bank(third, t, b):
-            if t % 2 == 0 and b == 0:
-                staged[third] = stage_pool.tile([P, 2 * THIRD], F32, name="staged", tag="staged")
-            qkv_banks[(t, b)] = new_bank([P, BANK], F32, "qkv_bank")
-
-        def second_pass(third, t, b, g):
-            cols = slice(BANK * b, BANK * (b + 1))
-            nc.tensor.matmul_mx(
-                out=qkv_banks[(t, b)][:],
-                lhsT=n_codes[:, g, t, :].bitcast(FP8X4),
-                lhsT_scale=n_scales[:, g, t, :],
-                rhs=up_codes[third][:, g, cols].bitcast(FP8X4),
-                rhs_scale=up_scales[third][:, g, cols],
-                start=(g == 0),
-                stop=(g == UP_PASSES - 1),
-            )
-
-        def drain(third, t, b, copy):
-            plain, rope = views(third)
-            if rope is not None and P * b >= NOPE:
-                target = rope[:, :, t % 2, :]
-            else:
-                target = plain[:, :, t % 2, P * b : P * (b + 1)]
-            copy(out=target, in_=qkv_banks[(t, b)][:].rearrange("p (d h) -> p h d", h=HEADS))
-
-        def second(third, t):
-            for b in range(BLOCKS):
-                open_bank(third, t, b)
+        def second(third, b, pair, copies):
+            if b == 0:
+                staged[(third, pair)] = stage_pool.tile([P, 2 * THIRD], F32, name="staged", tag="staged")
+            plain, rope = views(third, pair)
+            for tl in range(2):
+                t = 2 * pair + tl
+                bank = new_bank([P, BANK], F32, "qkv_bank")
                 for g in range(UP_PASSES):
-                    second_pass(third, t, b, g)
-                drain(third, t, b, nc.scalar.copy)
+                    nc.tensor.matmul_mx(
+                        out=bank[:],
+                        lhsT=n_codes[:, g, t, :].bitcast(FP8X4),
+                        lhsT_scale=n_scales[:, g, t, :],
+                        rhs=up_codes[(third, b)][:, g, :].bitcast(FP8X4),
+                        rhs_scale=up_scales[(third, b)][:, g, :],
+                        start=(g == 0),
+                        stop=(g == UP_PASSES - 1),
+                    )
+                if rope is not None and P * b >= NOPE:
+                    target = rope[:, :, tl, :]
+                else:
+                    target = plain[:, :, tl, P * b : P * (b + 1)]
+                copies[tl % len(copies)](out=target, in_=bank[:].rearrange("p (d h) -> p h d", h=HEADS))
 
         def store_plain(third, pair):
             tokens = slice(2 * pair, 2 * pair + 2)
             nc.sync.dma_start(
                 out=outputs[third][0][0].rearrange("h (p t) d -> p h t d", t=TOKEN_TILES)[:, :, tokens, :],
-                in_=views(third)[0],
+                in_=views(third, pair)[0],
             )
 
-        def rotate(rope, pair, rope_out):
+        def rotate(third, pair):
+            rope = views(third, pair)[1]
+            rope_out = outputs[third][1]
             tokens = slice(2 * pair, 2 * pair + 2)
             rotated = rope[:, :, :, 0:ROTATED]
             partner = rotated.rearrange("p h t (i e) -> p h t i e", e=2)
@@ -371,18 +386,23 @@ def tile_mhlattention_pa_kernel(tc, x, w_down, rms_w, w_up, out_0, out_1, out_2,
             down_scales = first_pool.tile([P, DOWN_PASSES, LATENT], U8, name="down_scales", align_bytes=64)
             x_codes = first_pool.tile([P, TOKEN_PAIRS, DOWN_PASSES, 2 * P], U32, name="x_codes", align_bytes=64)
             x_scales = first_pool.tile([P, TOKEN_PAIRS, DOWN_PASSES, 2 * P], U8, name="x_scales", align_bytes=64)
-            fetch(0)
-            fetch(1)
+            by_scalar = [nc.scalar.copy]
+            by_both = [nc.scalar.copy, nc.vector.tensor_copy]
+            fetch_next()
+            fetch_next()
             fetch_x(0)
             fetch_x(1)
-            fetch(2)
-            nc.sync.dma_start(out=gain[:], in_=rms_w.partition_broadcast(P))
+            fetch_next()
+            fetch_next()
             regroup(0)
             angles()
             step(0)
             quantise_x(0)
+            fetch_next()
             rope_tables()
             quantise_x(1)
+            fetch_next()
+            nc.sync.dma_start(out=gain[:], in_=rms_w.partition_broadcast(P))
             open_h_banks(0)
             for t in range(2):
                 for b in range(BLOCKS):
@@ -409,49 +429,28 @@ def tile_mhlattention_pa_kernel(tc, x, w_down, rms_w, w_up, out_0, out_1, out_2,
             squares(1)
             step(6)
             scale(1)
-            second(0, 0)
-            second(0, 1)
+            for b in range(BLOCKS):
+                second(V, b, 0, by_scalar)
+            store_plain(V, 0)
             flip(1)
             step(7)
             quantise_n(1)
-            store_plain(0, 0)
-            rotate(views(0)[1], 0, out_1)
-            second(0, 2)
-            step(8)
-            second(0, 3)
-            step(9)
-            store_plain(0, 1)
-            rotate(views(0)[1], 1, out_1)
-            second(1, 0)
-            second(1, 1)
-            store_plain(1, 0)
-            k_rope = {0: views(1)[1]}
-            step(10)
-            second(1, 2)
-            step(11)
-            second(1, 3)
-            store_plain(1, 1)
-            k_rope[1] = views(1)[1]
-            for t in range(2):
-                for b in range(BLOCKS):
-                    open_bank(2, t, b)
-                    for g in range(UP_PASSES - 1):
-                        second_pass(2, t, b, g)
-            step(12)
             for b in range(BLOCKS):
-                for t in range(2):
-                    second_pass(2, t, b, UP_PASSES - 1)
-            for t in range(2):
-                for b in range(BLOCKS):
-                    drain(2, t, b, nc.vector.tensor_copy if (t * BLOCKS + b) % 2 == 0 else nc.scalar.copy)
-            store_plain(2, 0)
-            rotate(k_rope[0], 0, out_3)
-            for t in range(2, TOKEN_TILES):
-                for b in range(BLOCKS):
-                    open_bank(2, t, b)
-                    for g in range(UP_PASSES):
-                        second_pass(2, t, b, g)
-                    drain(2, t, b, nc.vector.tensor_copy if (t * BLOCKS + b) % 2 == 0 else nc.scalar.copy)
-                if t == 2:
-                    rotate(k_rope[1], 1, out_3)
-            store_plain(2, 1)
+                second(V, b, 1, by_scalar)
+            store_plain(V, 1)
+            step(8)
+            for s in range(DOWN_PASSES + BLOCKS, STEPS):
+                place, b = divmod(s - DOWN_PASSES, BLOCKS)
+                third = TURN[place]
+                last = s + 1 == STEPS
+                for pair in range(TOKEN_PAIRS):
+                    second(third, b, pair, by_both if last else by_scalar)
+                    if b == 1:
+                        store_plain(third, pair)
+                    if last:
+                        rotate(third, pair)
+                if s + 2 < STEPS:
+                    step(s + 2)
+                if b == 2 and not last:
+                    rotate(third, 0)
+                    rotate(third, 1)

@@ -78,19 +78,28 @@ def tile_mhlattention_pa_kernel(tc, x, w_down, rms_w, w_up, out_0, out_1, out_2,
         trig = consts.tile([P, 2, PAIRS, TOKEN_TILES], F32, name="trig")
         cos_rep = consts.tile([P, TOKEN_TILES, PAIRS, 2], F32, name="cos_rep")
         sin_sign = consts.tile([P, TOKEN_TILES, 2, PAIRS], F32, name="sin_sign")
+        one = consts.tile([P, 1], F32, name="one")
+        one_root = consts.tile([P, 1], F32, name="one_root")
 
         def angles():
             nc.vector.tensor_copy(out=pos[:], in_=pos_int[:])
-            for i in range(PAIRS):
+            nc.vector.tensor_scalar_mul(out=turns[:, 0, 0, :], in0=pos[:], scalar1=1.0 / TWO_PI)
+            done = 1
+            while done < PAIRS:
                 nc.vector.tensor_scalar_mul(
-                    out=turns[:, 0, i, :], in0=pos[:], scalar1=10000.0 ** (-i / PAIRS) / TWO_PI
+                    out=turns[:, 0, done : 2 * done, :],
+                    in0=turns[:, 0, 0:done, :],
+                    scalar1=10000.0 ** (-done / PAIRS),
                 )
+                done *= 2
             nc.vector.tensor_scalar_add(out=turns[:, 1, :, :], in0=turns[:, 0, :, :], scalar1=0.25)
             nc.vector.tensor_scalar(
                 out=whole[:], in0=turns[:], scalar1=ROUND_MAGIC, scalar2=ROUND_MAGIC, op0=ALU.add, op1=ALU.subtract
             )
             nc.vector.tensor_tensor(out=frac[:], in0=turns[:], in1=whole[:], op=ALU.subtract)
             nc.scalar.activation(out=trig[:], in_=frac[:], func=ACT.Sin, scale=TWO_PI)
+            nc.vector.memset(one[:], 1.0)
+            nc.scalar.activation(out=one_root[:], in_=one[:], func=ACT.Sqrt)
 
         def rope_tables():
             nc.vector.tensor_copy(
@@ -320,16 +329,15 @@ def tile_mhlattention_pa_kernel(tc, x, w_down, rms_w, w_up, out_0, out_1, out_2,
                 whole_tile[:, split:].rearrange("p (h t d) -> p h t d", h=HEADS, t=2),
             )
 
-        def second(third, b, pair, copies):
-            if b == 0:
-                staged[(third, pair)] = stage_pool.tile([P, 2 * THIRD], F32, name="staged", tag="staged")
-            plain, rope = views(third, pair)
-            for tl in range(2):
-                t = 2 * pair + tl
-                bank = new_bank([P, BANK], F32, "qkv_bank")
-                for g in range(UP_PASSES):
+        def second(third, b, pairs, copies):
+            tiles = [2 * pair + tl for pair in pairs for tl in range(2)]
+            filled = {}
+            for t in tiles:
+                filled[t] = new_bank([P, BANK], F32, "qkv_bank")
+            for g in range(UP_PASSES):
+                for t in tiles:
                     nc.tensor.matmul_mx(
-                        out=bank[:],
+                        out=filled[t][:],
                         lhsT=n_codes[:, g, t, :].bitcast(FP8X4),
                         lhsT_scale=n_scales[:, g, t, :],
                         rhs=up_codes[(third, b)][:, g, :].bitcast(FP8X4),
@@ -337,11 +345,16 @@ def tile_mhlattention_pa_kernel(tc, x, w_down, rms_w, w_up, out_0, out_1, out_2,
                         start=(g == 0),
                         stop=(g == UP_PASSES - 1),
                     )
+            for t in tiles:
+                pair, tl = divmod(t, 2)
+                if b == 0 and tl == 0:
+                    staged[(third, pair)] = stage_pool.tile([P, 2 * THIRD], F32, name="staged", tag="staged")
+                plain, rope = views(third, pair)
                 if rope is not None and P * b >= NOPE:
                     target = rope[:, :, tl, :]
                 else:
                     target = plain[:, :, tl, P * b : P * (b + 1)]
-                copies[tl % len(copies)](out=target, in_=bank[:].rearrange("p (d h) -> p h d", h=HEADS))
+                copies[t % len(copies)](out=target, in_=filled[t][:].rearrange("p (d h) -> p h d", h=HEADS))
 
         def store_plain(third, pair):
             tokens = slice(2 * pair, 2 * pair + 2)
@@ -414,8 +427,8 @@ def tile_mhlattention_pa_kernel(tc, x, w_down, rms_w, w_up, out_0, out_1, out_2,
                         first_pass(t, b, g)
             squares(0)
             step(4)
+            regroup(6)
             scale(0)
-            flip(0)
             open_h_banks(1)
             for t in range(2, TOKEN_TILES):
                 for b in range(BLOCKS):
@@ -424,27 +437,29 @@ def tile_mhlattention_pa_kernel(tc, x, w_down, rms_w, w_up, out_0, out_1, out_2,
         with tc.tile_pool(name="stage", bufs=4, reuse_waits="tile") as stage_pool, tc.tile_pool(
             name="swap", bufs=2, reuse_waits="tile"
         ) as swap_pool:
-            step(5)
-            quantise_n(0)
+            quantise(5)
             squares(1)
-            step(6)
+            flip(0)
+            regroup(7)
             scale(1)
-            for b in range(BLOCKS):
-                second(V, b, 0, by_scalar)
-            store_plain(V, 0)
+            quantise_n(0)
             flip(1)
+            quantise(6)
+            for b in range(BLOCKS):
+                second(V, b, [0], by_scalar)
+            store_plain(V, 0)
             step(7)
             quantise_n(1)
             for b in range(BLOCKS):
-                second(V, b, 1, by_scalar)
+                second(V, b, [1], by_scalar)
             store_plain(V, 1)
             step(8)
             for s in range(DOWN_PASSES + BLOCKS, STEPS):
                 place, b = divmod(s - DOWN_PASSES, BLOCKS)
                 third = TURN[place]
                 last = s + 1 == STEPS
+                second(third, b, [0, 1], by_both if last else by_scalar)
                 for pair in range(TOKEN_PAIRS):
-                    second(third, b, pair, by_both if last else by_scalar)
                     if b == 1:
                         store_plain(third, pair)
                     if last:

from contextlib import ExitStack

import concourse.mybir as mybir
from concourse.masks import make_identity

F32 = mybir.dt.float32
BF16 = mybir.dt.bfloat16
I32 = mybir.dt.int32
U32 = mybir.dt.uint32
U8 = mybir.dt.uint8
FP8X4 = mybir.dt.float8_e4m3fn_x4
ALU = mybir.AluOpType
ACT = mybir.ActivationFunctionType
AXIS = mybir.AxisListType

P = 128
PACK = 4
K_PASS = P * PACK
BANK = 512
PSUM_BANKS = 8

TOKENS = 512
TOKEN_TILES = TOKENS // P
TOKEN_PAIRS = TOKEN_TILES // 2
D_MODEL = 2048
LATENT = 1536
HEADS = 4
NOPE = 256
ROPE = 128
ROTATED = 64
PAIRS = ROTATED // 2
D_HEAD = NOPE + ROPE
THIRD = HEADS * D_HEAD
THIRDS = 3
Q, K, V = 0, 1, 2
TURN = (V, Q, K)
EPS = 1e-6

DOWN_PASSES = D_MODEL // K_PASS
UP_PASSES = LATENT // K_PASS
BLOCKS = LATENT // BANK
LOADS = DOWN_PASSES + THIRDS * UP_PASSES
STEPS = LOADS
RAW_BUFS = 6
TWO_PI = 6.283185307179586
ROUND_MAGIC = 12582912.0

FLOPS = 2 * TOKENS * (D_MODEL * LATENT + LATENT * THIRDS * THIRD)


def tile_mhlattention_pa_kernel(tc, x, w_down, rms_w, w_up, out_0, out_1, out_2, out_3, out_4):
    nc = tc.nc
    with ExitStack() as pools:
        pools.enter_context(tc.manual_schedule())
        consts = pools.enter_context(tc.tile_pool(name="consts", bufs=1))
        raw_pool = pools.enter_context(tc.tile_pool(name="raw", bufs=RAW_BUFS))
        grouped_pool = pools.enter_context(tc.tile_pool(name="grouped", bufs=2 * BLOCKS))
        up_pool = pools.enter_context(tc.tile_pool(name="up", bufs=4))
        keep = pools.enter_context(tc.tile_pool(name="keep", bufs=1))
        norm_pool = pools.enter_context(tc.tile_pool(name="norm", bufs=2))
        banks = pools.enter_context(tc.psum_pool(name="banks", bufs=PSUM_BANKS))

        def new_bank(shape, dtype, name):
            return banks.tile(shape, dtype, name=name, tag="bank")

        ident_f32 = consts.tile([P, P], F32, name="ident_f32")
        make_identity(nc, ident_f32[:])
        ident_bf = consts.tile([P, P], BF16, name="ident_bf")
        make_identity(nc, ident_bf[:])
        gain = consts.tile([P, LATENT], BF16, name="gain")

        pos_int = consts.tile([P, TOKEN_TILES], I32, name="pos_int")
        nc.gpsimd.iota(pos_int[:], pattern=[[1, TOKEN_TILES]], base=0, channel_multiplier=TOKEN_TILES)
        pos = consts.tile([P, TOKEN_TILES], F32, name="pos")
        turns = consts.tile([P, 2, PAIRS, TOKEN_TILES], F32, name="turns")
        whole = consts.tile([P, 2, PAIRS, TOKEN_TILES], F32, name="whole")
        frac = consts.tile([P, 2, PAIRS, TOKEN_TILES], F32, name="frac")
        trig = consts.tile([P, 2, PAIRS, TOKEN_TILES], F32, name="trig")
        cos_rep = consts.tile([P, TOKEN_TILES, PAIRS, 2], F32, name="cos_rep")
        sin_sign = consts.tile([P, TOKEN_TILES, 2, PAIRS], F32, name="sin_sign")
        one = consts.tile([P, 1], F32, name="one")
        one_root = consts.tile([P, 1], F32, name="one_root")

        def angles():
            nc.vector.tensor_copy(out=pos[:], in_=pos_int[:])
            nc.vector.tensor_scalar_mul(out=turns[:, 0, 0, :], in0=pos[:], scalar1=1.0 / TWO_PI)
            done = 1
            while done < PAIRS:
                nc.vector.tensor_scalar_mul(
                    out=turns[:, 0, done : 2 * done, :],
                    in0=turns[:, 0, 0:done, :],
                    scalar1=10000.0 ** (-done / PAIRS),
                )
                done *= 2
            nc.vector.tensor_scalar_add(out=turns[:, 1, :, :], in0=turns[:, 0, :, :], scalar1=0.25)
            nc.vector.tensor_scalar(
                out=whole[:], in0=turns[:], scalar1=ROUND_MAGIC, scalar2=ROUND_MAGIC, op0=ALU.add, op1=ALU.subtract
            )
            nc.vector.tensor_tensor(out=frac[:], in0=turns[:], in1=whole[:], op=ALU.subtract)
            nc.scalar.activation(out=trig[:], in_=frac[:], func=ACT.Sin, scale=TWO_PI)
            nc.vector.memset(one[:], 1.0)
            nc.scalar.activation(out=one_root[:], in_=one[:], func=ACT.Sqrt)

        def rope_tables():
            nc.vector.tensor_copy(
                out=cos_rep[:],
                in_=trig[:, 1, :, :]
                .rearrange("p i t -> p t i")
                .unsqueeze(3)
                .to_broadcast([P, TOKEN_TILES, PAIRS, 2]),
            )
            nc.vector.tensor_scalar_mul(
                out=sin_sign[:, :, 0, :], in0=trig[:, 0, :, :].rearrange("p i t -> p t i"), scalar1=-1.0
            )
            nc.vector.tensor_copy(out=sin_sign[:, :, 1, :], in_=trig[:, 0, :, :].rearrange("p i t -> p t i"))

        n_grouped = keep.tile([P, UP_PASSES, TOKEN_TILES, P * PACK], BF16, name="n_grouped", align_bytes=64)
        n_codes = keep.tile([P, UP_PASSES, TOKEN_TILES, P], U32, name="n_codes", align_bytes=64)
        n_scales = keep.tile([P, UP_PASSES, TOKEN_TILES, P], U8, name="n_scales", align_bytes=64)
        sum_sq = keep.tile([P, TOKEN_TILES, BLOCKS], F32, name="sum_sq")
        sum_copy = keep.tile([P, TOKEN_TILES, BLOCKS], F32, name="sum_copy")
        total_sq = keep.tile([P, TOKEN_TILES], F32, name="total_sq")
        rms = keep.tile([P, TOKEN_TILES], F32, name="rms")
        rstd = keep.tile([P, TOKEN_TILES], F32, name="rstd")


        raw_rows = {}
        step_blocks = {}
        step_grouped = {}
        up_codes = {}
        up_scales = {}
        asked = [0]

        def fetch_next():
            load = asked[0]
            asked[0] += 1
            if load >= LOADS:
                return
            raw = raw_pool.tile([P, PACK, LATENT], BF16, name="raw", tag="raw")
            raw_rows[load] = raw
            if load < DOWN_PASSES:
                pieces = BLOCKS if load == 0 else 1
                width = LATENT // pieces
                for piece in range(pieces):
                    cols = slice(width * piece, width * (piece + 1))
                    for u in range(2):
                        rows = w_down[K_PASS * load + 256 * u : K_PASS * load + 256 * (u + 1), cols]
                        nc.sync.dma_start(
                            out=raw[:, 2 * u : 2 * u + 2, cols], in_=rows.rearrange("(q e) c -> q e c", e=2)
                        )
            else:
                place, g = divmod(load - DOWN_PASSES, UP_PASSES)
                third = TURN[place]
                rows = w_up[K_PASS * g : K_PASS * (g + 1), THIRD * third : THIRD * (third + 1)]
                nc.sync.dma_start(out=raw[:], in_=rows.rearrange("(j p) c -> p j c", p=P))

        def blocks_of(s):
            found = []
            if s < DOWN_PASSES:
                for b in range(BLOCKS):
                    cols = slice(BANK * b, BANK * (b + 1))
                    found.append((raw_rows[s][:, :, cols], down_codes[:, s, cols], down_scales[:, s, cols]))
                return found
            place, part = divmod(s - DOWN_PASSES, BLOCKS)
            third = TURN[place]
            for i in range(BLOCKS):
                g, b = (part, i) if place == 0 else (i, part)
                if (third, b) not in up_codes:
                    up_codes[(third, b)] = up_pool.tile(
                        [P, UP_PASSES, BANK], U32, name="up_codes", tag="up_codes", align_bytes=64
                    )
                    up_scales[(third, b)] = up_pool.tile(
                        [P, UP_PASSES, BANK], U8, name="up_scales", tag="up_scales", align_bytes=64
                    )
                raw = raw_rows[DOWN_PASSES + UP_PASSES * place + g]
                found.append(
                    (raw[:, :, BANK * b : BANK * (b + 1)], up_codes[(third, b)][:, g, :], up_scales[(third, b)][:, g, :])
                )
            return found

        def regroup(s):
            if s >= STEPS:
                return
            step_blocks[s] = blocks_of(s)
            step_grouped[s] = []
            for i in range(BLOCKS):
                grouped = grouped_pool.tile([P, BANK * PACK], BF16, name="grouped", tag="grouped", align_bytes=64)
                copy = nc.scalar.copy if i == BLOCKS - 1 else nc.vector.tensor_copy
                copy(
                    out=grouped[:].rearrange("p (c i t) -> p c t i", i=4, t=PACK),
                    in_=step_blocks[s][i][0].rearrange("p t (c i) -> p c t i", i=4),
                )
                step_grouped[s].append(grouped)
            if s < DOWN_PASSES + UP_PASSES:
                fetch_next()
            elif (s - DOWN_PASSES) % BLOCKS == BLOCKS - 1:
                for g in range(UP_PASSES):
                    fetch_next()

        def quantise(s):
            for i in range(BLOCKS):
                nc.vector.quantize_mx(
                    out=step_blocks[s][i][1].bitcast(FP8X4), scales=step_blocks[s][i][2], in_=step_grouped[s][i][:]
                )

        def step(s):
            regroup(s + 1)
            quantise(s)

        x_raw = {}

        def fetch_x(pair):
            x_raw[pair] = raw_pool.tile([P, 2, D_MODEL], BF16, name="x_raw", tag="raw")
            nc.sync.dma_start(
                out=x_raw[pair][:],
                in_=x[0].rearrange("(p t) k -> p t k", t=TOKEN_TILES)[:, 2 * pair : 2 * pair + 2, :],
            )

        def quantise_x(pair):
            for half in range(DOWN_PASSES // 2):
                x_grouped = grouped_pool.tile([P, BANK * PACK], BF16, name="x_grouped", tag="grouped", align_bytes=64)
                x_words = x_grouped[:].bitcast(F32).rearrange("q (g t u) -> q g t u", g=2, u=2)
                for gg in range(2):
                    g = 2 * half + gg
                    flipped = new_bank([P, 2, 2 * P], F32, "x_flipped")
                    for u in range(2):
                        for tl in range(2):
                            first_word = 256 * g + P * u
                            nc.tensor.transpose(
                                flipped[:, u, P * tl : P * (tl + 1)],
                                x_raw[pair][:, tl, :].bitcast(F32)[:, first_word : first_word + P],
                                ident_f32[:],
                            )
                    nc.scalar.copy(out=x_words[:, gg, :, :], in_=flipped[:].rearrange("q u t -> q t u"))
                passes = slice(2 * half, 2 * half + 2)
                nc.vector.quantize_mx(
                    out=x_codes[:, pair, passes, :].rearrange("q g t -> q (g t)").bitcast(FP8X4),
                    scales=x_scales[:, pair, passes, :].rearrange("q g t -> q (g t)"),
                    in_=x_grouped[:],
                )

        h_banks = {}

        def open_h_banks(pair):
            for t in (2 * pair, 2 * pair + 1):
                for b in range(BLOCKS):
                    h_banks[(t, b)] = new_bank([P, BANK], F32, "h_bank")

        def first_pass(t, b, g):
            pair, tl = divmod(t, 2)
            tok = slice(P * tl, P * (tl + 1))
            cols = slice(BANK * b, BANK * (b + 1))
            nc.tensor.matmul_mx(
                out=h_banks[(t, b)][:],
                lhsT=x_codes[:, pair, g, tok].bitcast(FP8X4),
                lhsT_scale=x_scales[:, pair, g, tok],
                rhs=down_codes[:, g, cols].bitcast(FP8X4),
                rhs_scale=down_scales[:, g, cols],
                start=(g == 0),
                stop=(g == DOWN_PASSES - 1),
            )

        def squares(pair):
            for t in (2 * pair, 2 * pair + 1):
                for b in range(BLOCKS):
                    unread = norm_pool.tile([P, BANK], BF16, name="unread", tag="unread", bufs=4)
                    nc.scalar.activation(
                        out=unread[:], in_=h_banks[(t, b)][:], func=ACT.Square, accum_out=sum_sq[:, t, b : b + 1]
                    )
                nc.scalar.activation(
                    out=sum_copy[:, t, :], in_=sum_sq[:, t, :], func=ACT.Copy, accum_out=total_sq[:, t : t + 1]
                )
            two = slice(2 * pair, 2 * pair + 2)
            nc.scalar.activation(out=rms[:, two], in_=total_sq[:, two], func=ACT.Sqrt, scale=1.0 / LATENT, bias=EPS)

        n_bf = {}

        def scale(pair):
            two = slice(2 * pair, 2 * pair + 2)
            nc.vector.reciprocal(out=rstd[:, two], in_=rms[:, two])
            for t in (2 * pair, 2 * pair + 1):
                n_bf[t] = norm_pool.tile([P, LATENT], BF16, name="n_bf", tag="n_bf", bufs=4)
                for b in range(BLOCKS):
                    cols = slice(BANK * b, BANK * (b + 1))
                    nc.vector.scalar_tensor_tensor(
                        out=n_bf[t][:, cols],
                        in0=h_banks[(t, b)][:],
                        scalar=rstd[:, t : t + 1],
                        in1=gain[:, cols],
                        op0=ALU.mult,
                        op1=ALU.mult,
                    )

        def flip(pair):
            for g in range(UP_PASSES):
                flipped = new_bank([P, 2, PACK, P], BF16, "n_flipped")
                for tl in range(2):
                    for j in range(PACK):
                        first_col = K_PASS * g + P * j
                        nc.tensor.transpose(
                            flipped[:, tl, j, :], n_bf[2 * pair + tl][:, first_col : first_col + P], ident_bf[:]
                        )
                nc.scalar.copy(
                    out=n_grouped[:, g, 2 * pair : 2 * pair + 2, :].rearrange("p t (r j) -> p t r j", j=PACK),
                    in_=flipped[:].rearrange("p t j r -> p t r j"),
                )

        def quantise_n(pair):
            two = slice(2 * pair, 2 * pair + 2)
            for g in range(UP_PASSES):
                nc.vector.quantize_mx(
                    out=n_codes[:, g, two, :].rearrange("p t r -> p (t r)").bitcast(FP8X4),
                    scales=n_scales[:, g, two, :].rearrange("p t r -> p (t r)"),
                    in_=n_grouped[:, g, two, :].rearrange("p t c -> p (t c)"),
                )

        outputs = [(out_0, out_1), (out_2, out_3), (out_4, None)]
        staged = {}
        split = 2 * HEADS * NOPE

        qkv_banks = {}

        def views(third, pair):
            whole_tile = staged[(third, pair)]
            if outputs[third][1] is None:
                return whole_tile[:].rearrange("p (h t d) -> p h t d", h=HEADS, t=2), None
            return (
                whole_tile[:, 0:split].rearrange("p (h t d) -> p h t d", h=HEADS, t=2),
                whole_tile[:, split:].rearrange("p (h t d) -> p h t d", h=HEADS, t=2),
            )

        def second(third, b, pairs, copies):
            tiles = [2 * pair + tl for pair in pairs for tl in range(2)]
            filled = {}
            for t in tiles:
                filled[t] = new_bank([P, BANK], F32, "qkv_bank")
            for g in range(UP_PASSES):
                for t in tiles:
                    nc.tensor.matmul_mx(
                        out=filled[t][:],
                        lhsT=n_codes[:, g, t, :].bitcast(FP8X4),
                        lhsT_scale=n_scales[:, g, t, :],
                        rhs=up_codes[(third, b)][:, g, :].bitcast(FP8X4),
                        rhs_scale=up_scales[(third, b)][:, g, :],
                        start=(g == 0),
                        stop=(g == UP_PASSES - 1),
                    )
            for t in tiles:
                pair, tl = divmod(t, 2)
                if b == 0 and tl == 0:
                    staged[(third, pair)] = stage_pool.tile([P, 2 * THIRD], F32, name="staged", tag="staged")
                plain, rope = views(third, pair)
                if rope is not None and P * b >= NOPE:
                    target = rope[:, :, tl, :]
                else:
                    target = plain[:, :, tl, P * b : P * (b + 1)]
                copies[t % len(copies)](out=target, in_=filled[t][:].rearrange("p (d h) -> p h d", h=HEADS))

        def store_plain(third, pair):
            tokens = slice(2 * pair, 2 * pair + 2)
            nc.sync.dma_start(
                out=outputs[third][0][0].rearrange("h (p t) d -> p h t d", t=TOKEN_TILES)[:, :, tokens, :],
                in_=views(third, pair)[0],
            )

        def rotate(third, pair):
            rope = views(third, pair)[1]
            rope_out = outputs[third][1]
            tokens = slice(2 * pair, 2 * pair + 2)
            rotated = rope[:, :, :, 0:ROTATED]
            partner = rotated.rearrange("p h t (i e) -> p h t i e", e=2)
            swapped = swap_pool.tile([P, HEADS, 2, 2, PAIRS], F32, name="swapped", tag="swapped")
            for e in range(2):
                nc.vector.tensor_tensor(
                    out=swapped[:, :, :, e, :],
                    in0=partner[:, :, :, :, 1 - e],
                    in1=sin_sign[:, tokens, e, :].unsqueeze(1).to_broadcast([P, HEADS, 2, PAIRS]),
                    op=ALU.mult,
                )
            nc.vector.tensor_tensor(
                out=rotated,
                in0=rotated,
                in1=cos_rep[:, tokens, :, :]
                .rearrange("p t i e -> p t (i e)")
                .unsqueeze(1)
                .to_broadcast([P, HEADS, 2, ROTATED]),
                op=ALU.mult,
            )
            rows = rotated.rearrange("p h t (i e) -> p (h t) i e", e=2)
            nc.vector.tensor_tensor(
                out=rows, in0=rows, in1=swapped[:].rearrange("p h t e i -> p (h t) i e"), op=ALU.add
            )
            nc.sync.dma_start(
                out=rope_out[0].rearrange("h (p t) d -> p h t d", t=TOKEN_TILES)[:, :, tokens, :], in_=rope
            )

        with tc.tile_pool(name="first", bufs=1) as first_pool:
            down_codes = first_pool.tile([P, DOWN_PASSES, LATENT], U32, name="down_codes", align_bytes=64)
            down_scales = first_pool.tile([P, DOWN_PASSES, LATENT], U8, name="down_scales", align_bytes=64)
            x_codes = first_pool.tile([P, TOKEN_PAIRS, DOWN_PASSES, 2 * P], U32, name="x_codes", align_bytes=64)
            x_scales = first_pool.tile([P, TOKEN_PAIRS, DOWN_PASSES, 2 * P], U8, name="x_scales", align_bytes=64)
            by_scalar = [nc.scalar.copy]
            by_both = [nc.scalar.copy, nc.vector.tensor_copy]
            fetch_next()
            fetch_next()
            fetch_x(0)
            fetch_x(1)
            fetch_next()
            fetch_next()
            regroup(0)
            angles()
            step(0)
            quantise_x(0)
            fetch_next()
            rope_tables()
            quantise_x(1)
            fetch_next()
            nc.sync.dma_start(out=gain[:], in_=rms_w.partition_broadcast(P))
            open_h_banks(0)
            for t in range(2):
                for b in range(BLOCKS):
                    first_pass(t, b, 0)
            for g in range(1, DOWN_PASSES):
                step(g)
                for t in range(2):
                    for b in range(BLOCKS):
                        first_pass(t, b, g)
            squares(0)
            step(4)
            regroup(6)
            scale(0)
            open_h_banks(1)
            for t in range(2, TOKEN_TILES):
                for b in range(BLOCKS):
                    for g in range(DOWN_PASSES):
                        first_pass(t, b, g)
        with tc.tile_pool(name="stage", bufs=4, reuse_waits="tile") as stage_pool, tc.tile_pool(
            name="swap", bufs=2, reuse_waits="tile"
        ) as swap_pool:
            quantise(5)
            squares(1)
            flip(0)
            regroup(7)
            scale(1)
            quantise_n(0)
            flip(1)
            quantise(6)
            for b in range(BLOCKS):
                second(V, b, [0], by_scalar)
            store_plain(V, 0)
            step(7)
            quantise_n(1)
            for b in range(BLOCKS):
                second(V, b, [1], by_scalar)
            store_plain(V, 1)
            step(8)
            for s in range(DOWN_PASSES + BLOCKS, STEPS):
                place, b = divmod(s - DOWN_PASSES, BLOCKS)
                third = TURN[place]
                last = s + 1 == STEPS
                second(third, b, [0, 1], by_both if last else by_scalar)
                for pair in range(TOKEN_PAIRS):
                    if b == 1:
                        store_plain(third, pair)
                    if last:
                        rotate(third, pair)
                if s + 2 < STEPS:
                    step(s + 2)
                if b == 2 and not last:
                    rotate(third, 0)
                    rotate(third, 1)
